import numpy as np
import ml_dtypes


def mxq(x, axis, fmt="e4m3"):
    dtype, down = {"e4m3": (ml_dtypes.float8_e4m3fn, 7), "e5m2": (ml_dtypes.float8_e5m2, 14)}[fmt]
    v = np.moveaxis(np.asarray(x, np.float32).astype(ml_dtypes.bfloat16).astype(np.float64), axis, -1)
    blocks = v.reshape(v.shape[:-1] + (-1, 32))
    amax = np.abs(blocks).max(-1, keepdims=True)
    byte = np.maximum(np.where(amax > 0, np.frexp(amax)[1] - 1 + 127, 0) - down, 1)
    scale = np.exp2(byte - 127.0)
    codes = (blocks / scale).astype(np.float32).astype(dtype).astype(np.float64)
    return np.moveaxis((codes * scale).reshape(v.shape), -1, axis)


WIDE = False


def mx_kscale(k):
    if not WIDE:
        return np.ones(k)
    levels = np.array([10, -10, 5, -5, 0])
    a = np.random.permutation(np.resize(levels, k // 512 * 4)).reshape(k // 512, 4)
    idx = np.arange(k)
    return np.exp2(a[idx // 512, idx % 128 // 32])


BF16 = ml_dtypes.bfloat16


def bf(x):
    return np.asarray(x, np.float32).astype(BF16)


def f64(x):
    return np.asarray(x).astype(np.float64)


B, S, D, QL, KL, H = 2, 256, 2048, 1536, 512, 16
HD = D // H
ROPE_BASE = 10000.0


def rope(x):
    d = x.shape[-1]
    half = d // 2
    inv_freq = 1.0 / (ROPE_BASE ** (np.arange(half, dtype=np.float64) * 2.0 / d))
    pos = np.arange(x.shape[1], dtype=np.float64)
    ang = pos[:, None] * inv_freq[None, :]
    cos = np.concatenate([np.cos(ang), np.cos(ang)], -1)[None]
    sin = np.concatenate([np.sin(ang), np.sin(ang)], -1)[None]
    x1, x2 = x[..., :half], x[..., half:]
    rot = np.concatenate([-x2, x1], -1)
    return x * cos + rot * sin


def setup_inputs():
    s, t = mx_kscale(D), mx_kscale(KL)
    return {"inputs_k": bf(np.random.standard_normal((B, S, D)) * s),
            "Wkv_down": bf(np.random.standard_normal((D, KL)) / np.sqrt(D) / s[:, None] * t),
            "Wk_up": bf(np.random.standard_normal((KL, D)) / np.sqrt(KL) / t[:, None]),
            "Wv_up": bf(np.random.standard_normal((KL, D)) / np.sqrt(KL) / t[:, None]),
            "Wk_rope": bf(np.random.standard_normal((D, HD)) / np.sqrt(D) / s[:, None])}


def reference(inputs_k, Wkv_down, Wk_up, Wv_up, Wk_rope):
    xq = mxq(f64(inputs_k), 2, "e4m3")
    kv_latent = xq @ mxq(f64(Wkv_down), 0, "e4m3")
    lq = mxq(kv_latent, 2, "e4m3")
    k_proj = (lq @ mxq(f64(Wk_up), 0, "e4m3")).reshape(B, S, H, HD)
    v_proj = (lq @ mxq(f64(Wv_up), 0, "e4m3")).reshape(B, S, H, HD)
    k_rope = rope(xq @ mxq(f64(Wk_rope), 0, "e4m3"))[:, :, None, :]
    k_new = np.concatenate([k_proj, np.broadcast_to(k_rope, (B, S, H, HD))], -1)
    return k_new, v_proj

@@ -1,0 +1,329 @@
+from contextlib import ExitStack
+
+import concourse.mybir as mybir
+from concourse.masks import make_identity
+
+F32 = mybir.dt.float32
+BF16 = mybir.dt.bfloat16
+I32 = mybir.dt.int32
+U32 = mybir.dt.uint32
+U8 = mybir.dt.uint8
+FP8X4 = mybir.dt.float8_e4m3fn_x4
+ALU = mybir.AluOpType
+ACT = mybir.ActivationFunctionType
+
+P = 128
+TOKENS = 512
+TT = 4
+D = 2048
+G = 4
+KL = 512
+HD = 128
+HEADS = 16
+ROPE_BASE = 10000.0
+PI = 3.141592653589793
+
+FLOPS = 2 * TOKENS * (D * KL + 2 * KL * D + D * HD)
+
+
+def round_bits(x, bits):
+    if x == 0.0:
+        return 0.0
+    s = 1.0
+    a = abs(x)
+    while a * s < 2.0 ** (bits - 1):
+        s *= 2.0
+    while a * s >= 2.0 ** bits:
+        s *= 0.5
+    return round(x * s) / s
+
+
+QUARTER_PI_1 = round_bits(PI / 4.0, 16)
+QUARTER_PI_2 = round_bits(PI / 4.0 - QUARTER_PI_1, 16)
+QUARTER_PI_3 = round_bits(PI / 4.0 - QUARTER_PI_1 - QUARTER_PI_2, 24)
+
+
+def tile_multiheadlatentattention_pb_kernel(tc, inputs_k, Wkv_down, Wk_up, Wv_up, Wk_rope, out_0, out_1):
+    nc = tc.nc
+    x = inputs_k.flatten_outer_dims()
+    k_out = out_0.rearrange("b s h d -> (b s) h d")
+    v_out = out_1.rearrange("b s h d -> (b s) (h d)")
+
+    with ExitStack() as ctx:
+        const = ctx.enter_context(tc.tile_pool(name="const", bufs=1))
+        raw = ctx.enter_context(tc.tile_pool(name="raw", bufs=1))
+        big = ctx.enter_context(tc.tile_pool(name="big", bufs=4))
+        grp = ctx.enter_context(tc.tile_pool(name="grp", bufs=4))
+        keep = ctx.enter_context(tc.tile_pool(name="keep", bufs=1))
+        stage = ctx.enter_context(tc.tile_pool(name="stage", bufs=1))
+        ps = ctx.enter_context(tc.psum_pool(name="ps", bufs=6))
+        psr = ctx.enter_context(tc.psum_pool(name="psr", bufs=1))
+
+        def vcopy(out, in_):
+            nc.vector.tensor_copy(out=out, in_=in_)
+
+        def scopy(out, in_):
+            nc.scalar.copy(out=out, in_=in_)
+
+        def quantise(codes, scales, in_):
+            nc.vector.quantize_mx(out=codes.bitcast(FP8X4), scales=scales, in_=in_)
+
+        def mx(out, a_codes, a_scales, b_codes, b_scales, start, stop):
+            nc.tensor.matmul_mx(
+                out=out,
+                lhsT=a_codes.bitcast(FP8X4),
+                lhsT_scale=a_scales,
+                rhs=b_codes.bitcast(FP8X4),
+                rhs_scale=b_scales,
+                start=start,
+                stop=stop,
+            )
+
+        wr_raw = raw.tile([P, G, 4 * HD], BF16)
+        nc.sync.dma_start(out=wr_raw[:], in_=Wk_rope.rearrange("(g p j) c -> p g (j c)", g=G, j=4))
+        wkr = [big.tile([P, 2, 4 * KL], BF16, tag="big", name="wkr%d" % i) for i in range(2)]
+        for g in range(G):
+            nc.sync.dma_start(
+                out=wkr[g // 2][:, g % 2, :],
+                in_=Wkv_down[512 * g : 512 * (g + 1), :].rearrange("(p j) c -> p (j c)", j=4),
+            )
+        xr = [big.tile([P, 2, D], BF16, tag="big", name="xr%d" % i) for i in range(2)]
+        for m in range(TT):
+            nc.sync.dma_start(out=xr[m // 2][:, m % 2, :], in_=x[P * m : P * (m + 1), :])
+        wu_raw = [raw.tile([P, 4, D], BF16, name="wu_raw%d" % w) for w in range(2)]
+        for w, w_up in enumerate((Wk_up, Wv_up)):
+            view = w_up.rearrange("(p j) n -> p j n", j=4)
+            for a in range(2):
+                nc.sync.dma_start(out=wu_raw[w][:, 2 * a : 2 * a + 2, :], in_=view[:, 2 * a : 2 * a + 2, :])
+
+        pos_i = const.tile([P, 2], I32)
+        nc.gpsimd.iota(pos_i[:], pattern=[[P, 2]], base=0, channel_multiplier=1)
+        ident = const.tile([P, P], F32)
+        make_identity(nc, ident[:])
+
+        warm = const.tile([P, 1], F32)
+        nc.vector.memset(warm[:], 0.0)
+        warm_out = const.tile([P, 1], F32)
+        nc.scalar.activation(out=warm_out[:], in_=warm[:], func=ACT.Sin)
+
+        half_freq = const.tile([P, 64], F32)
+        nc.vector.memset(half_freq[:, 0:1], 0.5)
+        for e in range(6):
+            w = 1 << e
+            nc.vector.tensor_scalar(
+                out=half_freq[:, w : 2 * w],
+                in0=half_freq[:, 0:w],
+                scalar1=ROPE_BASE ** (-w / 64.0),
+                scalar2=None,
+                op0=ALU.mult,
+            )
+        pos = const.tile([P, 2], F32)
+        nc.vector.tensor_copy(out=pos[:], in_=pos_i[:])
+        half_ang = const.tile([P, 2, 64], F32)
+        for h in range(2):
+            nc.vector.tensor_scalar(
+                out=half_ang[:, h, :], in0=half_freq[:], scalar1=pos[:, h : h + 1], scalar2=None, op0=ALU.mult
+            )
+        ha = half_ang[:].rearrange("p h j -> p (h j)")
+        turns = const.tile([P, 2, P], F32)
+        nc.vector.tensor_scalar(out=turns[:, 0, :], in0=ha, scalar1=1.0 / PI, scalar2=None, op0=ALU.mult)
+        nc.vector.tensor_scalar(out=turns[:, 1, :], in0=ha, scalar1=1.0 / PI, scalar2=-0.25, op0=ALU.mult, op1=ALU.add)
+        turns_i = const.tile([P, 2, P], I32)
+        nc.vector.tensor_copy(out=turns_i[:], in_=turns[:])
+        quarters = const.tile([P, 2, P], F32)
+        nc.vector.tensor_scalar(out=quarters[:, 0, :], in0=turns_i[:, 0, :], scalar1=4.0, scalar2=None, op0=ALU.mult)
+        nc.vector.tensor_scalar(
+            out=quarters[:, 1, :], in0=turns_i[:, 1, :], scalar1=4.0, scalar2=1.0, op0=ALU.mult, op1=ALU.add
+        )
+        red1 = const.tile([P, 2, P], F32)
+        nc.vector.scalar_tensor_tensor(
+            out=red1[:],
+            in0=quarters[:],
+            scalar=-QUARTER_PI_1,
+            in1=ha.unsqueeze(1).to_broadcast([P, 2, P]),
+            op0=ALU.mult,
+            op1=ALU.add,
+        )
+        red2 = const.tile([P, 2, P], F32)
+        nc.vector.scalar_tensor_tensor(
+            out=red2[:], in0=quarters[:], scalar=-QUARTER_PI_2, in1=red1[:], op0=ALU.mult, op1=ALU.add
+        )
+        red3 = const.tile([P, 2, P], F32)
+        nc.vector.scalar_tensor_tensor(
+            out=red3[:], in0=quarters[:], scalar=-QUARTER_PI_3, in1=red2[:], op0=ALU.mult, op1=ALU.add
+        )
+
+        sin_half = const.tile([P, 2, P], F32)
+        sin_sq = const.tile([P, 2, 2, 64], F32)
+        cos2 = const.tile([P, 2, 2, 64], F32)
+        sin2 = const.tile([P, 2, 2, 64], F32)
+
+        wr_grp = grp.tile([P, 2048], BF16, tag="grp", align_bytes=64)
+        scopy(
+            wr_grp[:].rearrange("p (g c j) -> p g c j", g=G, j=4),
+            wr_raw[:].rearrange("p g (j c) -> p g c j", j=4),
+        )
+        wrc = keep.tile([P, G * HD], U32, align_bytes=64)
+        wrs = keep.tile([P, G * HD], U8, align_bytes=64)
+        nc.scalar.activation(out=sin_half[:], in_=red3[:], func=ACT.Sin)
+        nc.scalar.activation(out=sin_sq[:].rearrange("p c h j -> p c (h j)"), in_=sin_half[:], func=ACT.Square)
+
+        wkc = [keep.tile([P, KL], U32, name="wkc%d" % g, align_bytes=64) for g in range(G)]
+        wks = [keep.tile([P, KL], U8, name="wks%d" % g, align_bytes=64) for g in range(G)]
+        w_grp = []
+
+        def wkv_regroup(g, copy):
+            gw = grp.tile([P, 2048], BF16, tag="grp", name="gw%d" % g, align_bytes=64)
+            w_grp.append(gw)
+            copy(
+                gw[:].rearrange("p (i q j) -> p q j i", i=4, j=4),
+                wkr[g // 2][:, g % 2, :].rearrange("p (j q i) -> p q j i", j=4, i=4),
+            )
+
+        def wkv_quant(g):
+            quantise(wkc[g][:], wks[g][:], w_grp[g][:])
+
+        wkv_regroup(0, vcopy)
+        wkv_regroup(1, scopy)
+        quantise(wrc[:], wrs[:], wr_grp[:])
+        wkv_quant(0)
+        wkv_regroup(2, vcopy)
+        wkv_regroup(3, scopy)
+        wkv_quant(1)
+        wkv_quant(2)
+        nc.vector.tensor_scalar(
+            out=cos2[:],
+            in0=sin_sq[:, 0, :, :].unsqueeze(2).to_broadcast([P, 2, 2, 64]),
+            scalar1=-2.0,
+            scalar2=1.0,
+            op0=ALU.mult,
+            op1=ALU.add,
+        )
+        nc.vector.tensor_scalar(
+            out=sin2[:, :, 0, :], in0=sin_sq[:, 1, :, :], scalar1=2.0, scalar2=-1.0, op0=ALU.mult, op1=ALU.add
+        )
+        nc.vector.tensor_scalar(
+            out=sin2[:, :, 1, :], in0=sin_sq[:, 1, :, :], scalar1=-2.0, scalar2=1.0, op0=ALU.mult, op1=ALU.add
+        )
+
+        xc = [keep.tile([P, G * P], U32, name="xc%d" % m, align_bytes=64) for m in range(TT)]
+        xs = [keep.tile([P, G * P], U8, name="xs%d" % m, align_bytes=64) for m in range(TT)]
+        lc = [keep.tile([P, P], U32, name="lc%d" % m, align_bytes=64) for m in range(TT)]
+        ls = [keep.tile([P, P], U8, name="ls%d" % m, align_bytes=64) for m in range(TT)]
+        r_ps = [psr.tile([P, 2 * HD], F32, name="r_ps%d" % b) for b in range(2)]
+        rope = [const.tile([P, 2 * HD], F32, name="rope%d" % b) for b in range(2)]
+        x_grp = []
+        l_grp = []
+
+        def x_in(m):
+            xw = xr[m // 2][:, m % 2, :].bitcast(F32)
+            gx = grp.tile([P, 2048], BF16, tag="grp", name="gx%d" % m, align_bytes=64)
+            x_grp.append(gx)
+            gxw = gx[:].bitcast(F32).rearrange("p (g r u) -> p g r u", g=G, u=2)
+            for gp in range(2):
+                xt = ps.tile([P, 4, P], F32, tag="acc", name="xt")
+                for gi in range(2):
+                    g = 2 * gp + gi
+                    for u in range(2):
+                        nc.tensor.transpose(xt[:, 2 * gi + u, :], xw[:, 256 * g + u : 256 * (g + 1) : 2], ident[:])
+                (scopy if gp == 0 else vcopy)(
+                    gxw[:, 2 * gp : 2 * gp + 2, :, :], xt[:].rearrange("p (g u) r -> p g r u", u=2)
+                )
+
+        def x_quant(m):
+            quantise(xc[m][:], xs[m][:], x_grp[m][:])
+
+        def first_stage(m):
+            lat = ps.tile([P, 4, P], F32, tag="acc", name="lat")
+            for t in range(4):
+                ts = slice(P * t, P * (t + 1))
+                for g in range(G):
+                    gs = slice(P * g, P * (g + 1))
+                    mx(lat[:, t, :], wkc[g][:, ts], wks[g][:, ts], xc[m][:, gs], xs[m][:, gs], g == 0, g == G - 1)
+            hs = slice(HD * (m % 2), HD * (m % 2 + 1))
+            for g in range(G):
+                gs = slice(P * g, P * (g + 1))
+                mx(r_ps[m // 2][:, hs], xc[m][:, gs], xs[m][:, gs], wrc[:, gs], wrs[:, gs], g == 0, g == G - 1)
+            gl = stage.tile([P, 4 * P], BF16, name="gl%d" % m, align_bytes=64)
+            l_grp.append(gl)
+            scopy(gl[:].rearrange("p (r t) -> p r t", t=4), lat[:].rearrange("p t r -> p r t"))
+
+        def lat_quant(m):
+            quantise(lc[m][:], ls[m][:], l_grp[m][:])
+
+        def rotate(b):
+            t1 = const.tile([P, 2 * HD], F32, name="t1_%d" % b)
+            t2 = const.tile([P, 2, 2, 64], F32, name="t2_%d" % b)
+            rv = r_ps[b][:].rearrange("p (h f j) -> p h f j", h=2, f=2)
+            nc.vector.tensor_tensor(
+                out=t1[:], in0=r_ps[b][:], in1=cos2[:].rearrange("p h f j -> p (h f j)"), op=ALU.mult
+            )
+            for f in range(2):
+                nc.vector.tensor_tensor(out=t2[:, :, f, :], in0=rv[:, :, 1 - f, :], in1=sin2[:, :, f, :], op=ALU.mult)
+            nc.vector.tensor_tensor(
+                out=rope[b][:], in0=t1[:], in1=t2[:].rearrange("p h f j -> p (h f j)"), op=ALU.add
+            )
+
+        wuc = [keep.tile([P, 512], U32, name="wuc%d" % c, align_bytes=64) for c in range(8)]
+        wus = [keep.tile([P, 512], U8, name="wus%d" % c, align_bytes=64) for c in range(8)]
+        u_grp = []
+
+        def up_regroup(c, copy):
+            gu = grp.tile([P, 2048], BF16, tag="grp", name="gu%d" % c, align_bytes=64)
+            u_grp.append(gu)
+            cc = c % 4
+            copy(
+                gu[:].rearrange("p (c i j) -> p c j i", i=4, j=4),
+                wu_raw[c // 4][:, :, 512 * cc : 512 * (cc + 1)].rearrange("p j (c i) -> p c j i", i=4),
+            )
+
+        def up_quant(c):
+            quantise(wuc[c][:], wus[c][:], u_grp[c][:])
+
+        x_in(0)
+        wkv_quant(3)
+        x_in(1)
+        x_quant(0)
+        x_in(2)
+        x_quant(1)
+        first_stage(0)
+        x_in(3)
+        x_quant(2)
+        first_stage(1)
+        lat_quant(0)
+        x_quant(3)
+        first_stage(2)
+        lat_quant(1)
+        rotate(0)
+        first_stage(3)
+        up_regroup(0, vcopy)
+        lat_quant(2)
+        up_quant(0)
+        lat_quant(3)
+        rotate(1)
+
+        vst = []
+        for c in range(8):
+            if c + 1 < 8:
+                up_regroup(c + 1, vcopy)
+            for m in range(TT):
+                rows = slice(P * m, P * (m + 1))
+                o = ps.tile([P, 512], F32, tag="acc", name="o")
+                mx(o[:], lc[m][:], ls[m][:], wuc[c][:], wus[c][:], True, True)
+                if c < 4:
+                    hs = slice(HD * (m % 2), HD * (m % 2 + 1))
+                    kst = stage.tile([P, 4, 2 * HD], F32, name="kst%d_%d" % (c, m))
+                    (scopy if m < 2 else vcopy)(
+                        kst[:, :, HD : 2 * HD], rope[m // 2][:, hs].unsqueeze(1).to_broadcast([P, 4, HD])
+                    )
+                    scopy(kst[:, :, 0:HD], o[:].rearrange("p (h d) -> p h d", h=4))
+                    nc.sync.dma_start(out=k_out[rows, 4 * c : 4 * c + 4, :], in_=kst[:])
+                else:
+                    if c == 4:
+                        vst.append(big.tile([P, D], F32, tag="big", name="vst%d" % m))
+                    cc = c - 4
+                    (scopy if m < 3 else vcopy)(vst[m][:, 512 * cc : 512 * (cc + 1)], o[:])
+                    if c == 7:
+                        nc.sync.dma_start(out=v_out[rows, :], in_=vst[m][:])
+            if c + 1 < 8:
+                up_quant(c + 1)

@@ -50,6 +50,7 @@ def tile_multiheadlatentattention_pb_kernel(tc, inputs_k, Wkv_down, Wk_up, Wv_up
     v_out = out_1.rearrange("b s h d -> (b s) (h d)")
 
     with ExitStack() as ctx:
+        ctx.enter_context(tc.manual_schedule())
         const = ctx.enter_context(tc.tile_pool(name="const", bufs=1))
         raw = ctx.enter_context(tc.tile_pool(name="raw", bufs=1))
         big = ctx.enter_context(tc.tile_pool(name="big", bufs=4))
@@ -165,8 +166,6 @@ def tile_multiheadlatentattention_pb_kernel(tc, inputs_k, Wkv_down, Wk_up, Wv_up
         )
         wrc = keep.tile([P, G * HD], U32, align_bytes=64)
         wrs = keep.tile([P, G * HD], U8, align_bytes=64)
-        nc.scalar.activation(out=sin_half[:], in_=red3[:], func=ACT.Sin)
-        nc.scalar.activation(out=sin_sq[:].rearrange("p c h j -> p c (h j)"), in_=sin_half[:], func=ACT.Square)
 
         wkc = [keep.tile([P, KL], U32, name="wkc%d" % g, align_bytes=64) for g in range(G)]
         wks = [keep.tile([P, KL], U8, name="wks%d" % g, align_bytes=64) for g in range(G)]
@@ -188,23 +187,27 @@ def tile_multiheadlatentattention_pb_kernel(tc, inputs_k, Wkv_down, Wk_up, Wv_up
         quantise(wrc[:], wrs[:], wr_grp[:])
         wkv_quant(0)
         wkv_regroup(2, vcopy)
+        nc.scalar.activation(out=sin_half[:], in_=red3[:], func=ACT.Sin)
+        nc.scalar.activation(out=sin_sq[:].rearrange("p c h j -> p c (h j)"), in_=sin_half[:], func=ACT.Square)
         wkv_regroup(3, scopy)
         wkv_quant(1)
         wkv_quant(2)
-        nc.vector.tensor_scalar(
-            out=cos2[:],
-            in0=sin_sq[:, 0, :, :].unsqueeze(2).to_broadcast([P, 2, 2, 64]),
-            scalar1=-2.0,
-            scalar2=1.0,
-            op0=ALU.mult,
-            op1=ALU.add,
-        )
-        nc.vector.tensor_scalar(
-            out=sin2[:, :, 0, :], in0=sin_sq[:, 1, :, :], scalar1=2.0, scalar2=-1.0, op0=ALU.mult, op1=ALU.add
-        )
-        nc.vector.tensor_scalar(
-            out=sin2[:, :, 1, :], in0=sin_sq[:, 1, :, :], scalar1=-2.0, scalar2=1.0, op0=ALU.mult, op1=ALU.add
-        )
+
+        def finish_tables():
+            nc.vector.tensor_scalar(
+                out=cos2[:],
+                in0=sin_sq[:, 0, :, :].unsqueeze(2).to_broadcast([P, 2, 2, 64]),
+                scalar1=-2.0,
+                scalar2=1.0,
+                op0=ALU.mult,
+                op1=ALU.add,
+            )
+            nc.vector.tensor_scalar(
+                out=sin2[:, :, 0, :], in0=sin_sq[:, 1, :, :], scalar1=2.0, scalar2=-1.0, op0=ALU.mult, op1=ALU.add
+            )
+            nc.vector.tensor_scalar(
+                out=sin2[:, :, 1, :], in0=sin_sq[:, 1, :, :], scalar1=-2.0, scalar2=1.0, op0=ALU.mult, op1=ALU.add
+            )
 
         xc = [keep.tile([P, G * P], U32, name="xc%d" % m, align_bytes=64) for m in range(TT)]
         xs = [keep.tile([P, G * P], U8, name="xs%d" % m, align_bytes=64) for m in range(TT)]
@@ -284,27 +287,29 @@ def tile_multiheadlatentattention_pb_kernel(tc, inputs_k, Wkv_down, Wk_up, Wv_up
         wkv_quant(3)
         x_in(1)
         x_quant(0)
+        finish_tables()
         x_in(2)
         x_quant(1)
-        first_stage(0)
         x_in(3)
         x_quant(2)
+        first_stage(0)
+        x_quant(3)
         first_stage(1)
         lat_quant(0)
-        x_quant(3)
+        up_regroup(0, vcopy)
         first_stage(2)
         lat_quant(1)
         rotate(0)
-        first_stage(3)
-        up_regroup(0, vcopy)
-        lat_quant(2)
         up_quant(0)
+        first_stage(3)
+        lat_quant(2)
+        up_regroup(1, vcopy)
         lat_quant(3)
         rotate(1)
 
         vst = []
         for c in range(8):
-            if c + 1 < 8:
+            if 0 < c < 7:
                 up_regroup(c + 1, vcopy)
             for m in range(TT):
                 rows = slice(P * m, P * (m + 1))
@@ -323,7 +328,8 @@ def tile_multiheadlatentattention_pb_kernel(tc, inputs_k, Wkv_down, Wk_up, Wv_up
                         vst.append(big.tile([P, D], F32, tag="big", name="vst%d" % m))
                     cc = c - 4
                     (scopy if m < 3 else vcopy)(vst[m][:, 512 * cc : 512 * (cc + 1)], o[:])
-                    if c == 7:
-                        nc.sync.dma_start(out=v_out[rows, :], in_=vst[m][:])
+                    if c % 2 == 1:
+                        half = slice(1024 * (cc // 2), 1024 * (cc // 2 + 1))
+                        nc.sync.dma_start(out=v_out[rows, half], in_=vst[m][:, half])
             if c + 1 < 8:
                 up_quant(c + 1)

@@ -81,21 +81,39 @@ def tile_multiheadlatentattention_pb_kernel(tc, inputs_k, Wkv_down, Wk_up, Wv_up
             )
 
         wr_raw = raw.tile([P, G, 4 * HD], BF16)
-        nc.sync.dma_start(out=wr_raw[:], in_=Wk_rope.rearrange("(g p j) c -> p g (j c)", g=G, j=4))
         wkr = [big.tile([P, 2, 4 * KL], BF16, tag="big", name="wkr%d" % i) for i in range(2)]
-        for g in range(G):
+        xr = [big.tile([P, 2, D], BF16, tag="big", name="xr%d" % i) for i in range(2)]
+        wu_raw = [raw.tile([P, 4, D], BF16, name="wu_raw%d" % w) for w in range(2)]
+
+        def load_wr():
+            nc.sync.dma_start(out=wr_raw[:], in_=Wk_rope.rearrange("(g p j) c -> p g (j c)", g=G, j=4))
+
+        def load_wkv(g):
             nc.sync.dma_start(
                 out=wkr[g // 2][:, g % 2, :],
                 in_=Wkv_down[512 * g : 512 * (g + 1), :].rearrange("(p j) c -> p (j c)", j=4),
             )
-        xr = [big.tile([P, 2, D], BF16, tag="big", name="xr%d" % i) for i in range(2)]
-        for m in range(TT):
+
+        def load_x(m):
             nc.sync.dma_start(out=xr[m // 2][:, m % 2, :], in_=x[P * m : P * (m + 1), :])
-        wu_raw = [raw.tile([P, 4, D], BF16, name="wu_raw%d" % w) for w in range(2)]
-        for w, w_up in enumerate((Wk_up, Wv_up)):
-            view = w_up.rearrange("(p j) n -> p j n", j=4)
-            for a in range(2):
-                nc.sync.dma_start(out=wu_raw[w][:, 2 * a : 2 * a + 2, :], in_=view[:, 2 * a : 2 * a + 2, :])
+
+        def load_up(w, a):
+            view = (Wk_up, Wv_up)[w].rearrange("(p j) n -> p j n", j=4)
+            nc.sync.dma_start(out=wu_raw[w][:, 2 * a : 2 * a + 2, :], in_=view[:, 2 * a : 2 * a + 2, :])
+
+        load_wr()
+        load_wkv(0)
+        load_wkv(1)
+        load_wkv(2)
+        load_wkv(3)
+        load_x(0)
+        load_x(1)
+        load_x(2)
+        load_x(3)
+        load_up(0, 0)
+        load_up(0, 1)
+        load_up(1, 0)
+        load_up(1, 1)
 
         pos_i = const.tile([P, 2], I32)
         nc.gpsimd.iota(pos_i[:], pattern=[[P, 2]], base=0, channel_multiplier=1)
@@ -159,21 +177,26 @@ def tile_multiheadlatentattention_pb_kernel(tc, inputs_k, Wkv_down, Wk_up, Wv_up
         cos2 = const.tile([P, 2, 2, 64], F32)
         sin2 = const.tile([P, 2, 2, 64], F32)
 
-        wr_grp = grp.tile([P, 2048], BF16, tag="grp", align_bytes=64)
-        scopy(
-            wr_grp[:].rearrange("p (g c j) -> p g c j", g=G, j=4),
-            wr_raw[:].rearrange("p g (j c) -> p g c j", j=4),
-        )
+        wr_grp = keep.tile([P, 2048], BF16, align_bytes=64)
         wrc = keep.tile([P, G * HD], U32, align_bytes=64)
         wrs = keep.tile([P, G * HD], U8, align_bytes=64)
 
+        def wr_regroup(copy):
+            copy(
+                wr_grp[:].rearrange("p (g c j) -> p g c j", g=G, j=4),
+                wr_raw[:].rearrange("p g (j c) -> p g c j", j=4),
+            )
+
+        def wr_quant():
+            quantise(wrc[:], wrs[:], wr_grp[:])
+
         wkc = [keep.tile([P, KL], U32, name="wkc%d" % g, align_bytes=64) for g in range(G)]
         wks = [keep.tile([P, KL], U8, name="wks%d" % g, align_bytes=64) for g in range(G)]
-        w_grp = []
+        w_grp = {}
 
         def wkv_regroup(g, copy):
             gw = grp.tile([P, 2048], BF16, tag="grp", name="gw%d" % g, align_bytes=64)
-            w_grp.append(gw)
+            w_grp[g] = gw
             copy(
                 gw[:].rearrange("p (i q j) -> p q j i", i=4, j=4),
                 wkr[g // 2][:, g % 2, :].rearrange("p (j q i) -> p q j i", j=4, i=4),
@@ -182,16 +205,9 @@ def tile_multiheadlatentattention_pb_kernel(tc, inputs_k, Wkv_down, Wk_up, Wv_up
         def wkv_quant(g):
             quantise(wkc[g][:], wks[g][:], w_grp[g][:])
 
-        wkv_regroup(0, vcopy)
-        wkv_regroup(1, scopy)
-        quantise(wrc[:], wrs[:], wr_grp[:])
-        wkv_quant(0)
-        wkv_regroup(2, vcopy)
-        nc.scalar.activation(out=sin_half[:], in_=red3[:], func=ACT.Sin)
-        nc.scalar.activation(out=sin_sq[:].rearrange("p c h j -> p c (h j)"), in_=sin_half[:], func=ACT.Square)
-        wkv_regroup(3, scopy)
-        wkv_quant(1)
-        wkv_quant(2)
+        def trig():
+            nc.scalar.activation(out=sin_half[:], in_=red3[:], func=ACT.Sin)
+            nc.scalar.activation(out=sin_sq[:].rearrange("p c h j -> p c (h j)"), in_=sin_half[:], func=ACT.Square)
 
         def finish_tables():
             nc.vector.tensor_scalar(
@@ -215,13 +231,13 @@ def tile_multiheadlatentattention_pb_kernel(tc, inputs_k, Wkv_down, Wk_up, Wv_up
         ls = [keep.tile([P, P], U8, name="ls%d" % m, align_bytes=64) for m in range(TT)]
         r_ps = [psr.tile([P, 2 * HD], F32, name="r_ps%d" % b) for b in range(2)]
         rope = [const.tile([P, 2 * HD], F32, name="rope%d" % b) for b in range(2)]
-        x_grp = []
-        l_grp = []
+        x_grp = {}
+        l_grp = {}
 
-        def x_in(m):
+        def x_in(m, copies):
             xw = xr[m // 2][:, m % 2, :].bitcast(F32)
             gx = grp.tile([P, 2048], BF16, tag="grp", name="gx%d" % m, align_bytes=64)
-            x_grp.append(gx)
+            x_grp[m] = gx
             gxw = gx[:].bitcast(F32).rearrange("p (g r u) -> p g r u", g=G, u=2)
             for gp in range(2):
                 xt = ps.tile([P, 4, P], F32, tag="acc", name="xt")
@@ -229,27 +245,27 @@ def tile_multiheadlatentattention_pb_kernel(tc, inputs_k, Wkv_down, Wk_up, Wv_up
                     g = 2 * gp + gi
                     for u in range(2):
                         nc.tensor.transpose(xt[:, 2 * gi + u, :], xw[:, 256 * g + u : 256 * (g + 1) : 2], ident[:])
-                (scopy if gp == 0 else vcopy)(
-                    gxw[:, 2 * gp : 2 * gp + 2, :, :], xt[:].rearrange("p (g u) r -> p g r u", u=2)
-                )
+                copies[gp](gxw[:, 2 * gp : 2 * gp + 2, :, :], xt[:].rearrange("p (g u) r -> p g r u", u=2))
 
         def x_quant(m):
             quantise(xc[m][:], xs[m][:], x_grp[m][:])
 
-        def first_stage(m):
+        def first_stage(m, copy):
             lat = ps.tile([P, 4, P], F32, tag="acc", name="lat")
             for t in range(4):
                 ts = slice(P * t, P * (t + 1))
                 for g in range(G):
                     gs = slice(P * g, P * (g + 1))
                     mx(lat[:, t, :], wkc[g][:, ts], wks[g][:, ts], xc[m][:, gs], xs[m][:, gs], g == 0, g == G - 1)
+            gl = stage.tile([P, 4 * P], BF16, name="gl%d" % m, align_bytes=64)
+            l_grp[m] = gl
+            copy(gl[:].rearrange("p (r t) -> p r t", t=4), lat[:].rearrange("p t r -> p r t"))
+
+        def rope_stage(m):
             hs = slice(HD * (m % 2), HD * (m % 2 + 1))
             for g in range(G):
                 gs = slice(P * g, P * (g + 1))
                 mx(r_ps[m // 2][:, hs], xc[m][:, gs], xs[m][:, gs], wrc[:, gs], wrs[:, gs], g == 0, g == G - 1)
-            gl = stage.tile([P, 4 * P], BF16, name="gl%d" % m, align_bytes=64)
-            l_grp.append(gl)
-            scopy(gl[:].rearrange("p (r t) -> p r t", t=4), lat[:].rearrange("p t r -> p r t"))
 
         def lat_quant(m):
             quantise(lc[m][:], ls[m][:], l_grp[m][:])
@@ -269,11 +285,11 @@ def tile_multiheadlatentattention_pb_kernel(tc, inputs_k, Wkv_down, Wk_up, Wv_up
 
         wuc = [keep.tile([P, 512], U32, name="wuc%d" % c, align_bytes=64) for c in range(8)]
         wus = [keep.tile([P, 512], U8, name="wus%d" % c, align_bytes=64) for c in range(8)]
-        u_grp = []
+        u_grp = {}
 
         def up_regroup(c, copy):
             gu = grp.tile([P, 2048], BF16, tag="grp", name="gu%d" % c, align_bytes=64)
-            u_grp.append(gu)
+            u_grp[c] = gu
             cc = c % 4
             copy(
                 gu[:].rearrange("p (c i j) -> p c j i", i=4, j=4),
@@ -283,53 +299,82 @@ def tile_multiheadlatentattention_pb_kernel(tc, inputs_k, Wkv_down, Wk_up, Wv_up
         def up_quant(c):
             quantise(wuc[c][:], wus[c][:], u_grp[c][:])
 
-        x_in(0)
+        vst = {}
+        kst = [[stage.tile([P, 4, 2 * HD], F32, name="kst%d_%d" % (m, par)) for par in range(2)] for m in range(TT)]
+
+        def fill(m, par, copy):
+            hs = slice(HD * (m % 2), HD * (m % 2 + 1))
+            copy(kst[m][par][:, :, HD : 2 * HD], rope[m // 2][:, hs].unsqueeze(1).to_broadcast([P, 4, HD]))
+
+        def out_k(c, m, copy):
+            rows = slice(P * m, P * (m + 1))
+            o = ps.tile([P, 512], F32, tag="acc", name="o")
+            mx(o[:], lc[m][:], ls[m][:], wuc[c][:], wus[c][:], True, True)
+            copy(kst[m][c % 2][:, :, 0:HD], o[:].rearrange("p (h d) -> p h d", h=4))
+            nc.sync.dma_start(out=k_out[rows, 4 * c : 4 * c + 4, :], in_=kst[m][c % 2][:])
+
+        def out_v(c, m, copy):
+            rows = slice(P * m, P * (m + 1))
+            o = ps.tile([P, 512], F32, tag="acc", name="o")
+            mx(o[:], lc[m][:], ls[m][:], wuc[c][:], wus[c][:], True, True)
+            if c == 4:
+                vst[m] = big.tile([P, D], F32, tag="big", name="vst%d" % m)
+            cc = c - 4
+            copy(vst[m][:, 512 * cc : 512 * (cc + 1)], o[:])
+            if c % 2 == 1:
+                half = slice(1024 * (cc // 2), 1024 * (cc // 2 + 1))
+                nc.sync.dma_start(out=v_out[rows, half], in_=vst[m][:, half])
+
+        wr_regroup(scopy)
+        wkv_regroup(0, vcopy)
+        wkv_regroup(1, scopy)
+        wr_quant()
+        wkv_quant(0)
+        wkv_regroup(2, vcopy)
+        trig()
+        wkv_regroup(3, scopy)
+        wkv_quant(1)
+        wkv_quant(2)
+        x_in(0, (scopy, vcopy))
         wkv_quant(3)
-        x_in(1)
+        x_in(1, (scopy, vcopy))
         x_quant(0)
         finish_tables()
-        x_in(2)
+        x_in(2, (scopy, vcopy))
         x_quant(1)
-        x_in(3)
+        x_in(3, (scopy, vcopy))
         x_quant(2)
-        first_stage(0)
+        first_stage(0, scopy)
+        rope_stage(0)
         x_quant(3)
-        first_stage(1)
+        first_stage(1, scopy)
+        rope_stage(1)
         lat_quant(0)
         up_regroup(0, vcopy)
-        first_stage(2)
+        first_stage(2, scopy)
+        rope_stage(2)
         lat_quant(1)
         rotate(0)
         up_quant(0)
-        first_stage(3)
+        first_stage(3, scopy)
+        rope_stage(3)
         lat_quant(2)
         up_regroup(1, vcopy)
         lat_quant(3)
+        fill(0, 0, scopy)
+        fill(1, 0, scopy)
         rotate(1)
-
-        vst = []
+        fill(2, 0, vcopy)
+        fill(3, 0, vcopy)
         for c in range(8):
             if 0 < c < 7:
                 up_regroup(c + 1, vcopy)
             for m in range(TT):
-                rows = slice(P * m, P * (m + 1))
-                o = ps.tile([P, 512], F32, tag="acc", name="o")
-                mx(o[:], lc[m][:], ls[m][:], wuc[c][:], wus[c][:], True, True)
                 if c < 4:
-                    hs = slice(HD * (m % 2), HD * (m % 2 + 1))
-                    kst = stage.tile([P, 4, 2 * HD], F32, name="kst%d_%d" % (c, m))
-                    (scopy if m < 2 else vcopy)(
-                        kst[:, :, HD : 2 * HD], rope[m // 2][:, hs].unsqueeze(1).to_broadcast([P, 4, HD])
-                    )
-                    scopy(kst[:, :, 0:HD], o[:].rearrange("p (h d) -> p h d", h=4))
-                    nc.sync.dma_start(out=k_out[rows, 4 * c : 4 * c + 4, :], in_=kst[:])
+                    out_k(c, m, scopy)
                 else:
-                    if c == 4:
-                        vst.append(big.tile([P, D], F32, tag="big", name="vst%d" % m))
-                    cc = c - 4
-                    (scopy if m < 3 else vcopy)(vst[m][:, 512 * cc : 512 * (cc + 1)], o[:])
-                    if c % 2 == 1:
-                        half = slice(1024 * (cc // 2), 1024 * (cc // 2 + 1))
-                        nc.sync.dma_start(out=v_out[rows, half], in_=vst[m][:, half])
+                    out_v(c, m, scopy if m < 3 else vcopy)
+                if c == 0:
+                    fill(m, 1, scopy if m < 2 else vcopy)
             if c + 1 < 8:
                 up_quant(c + 1)

@@ -97,9 +97,12 @@ def tile_multiheadlatentattention_pb_kernel(tc, inputs_k, Wkv_down, Wk_up, Wv_up
         def load_x(m):
             nc.sync.dma_start(out=xr[m // 2][:, m % 2, :], in_=x[P * m : P * (m + 1), :])
 
-        def load_up(w, a):
+        def load_up_cols(w, c0, c1):
             view = (Wk_up, Wv_up)[w].rearrange("(p j) n -> p j n", j=4)
-            nc.sync.dma_start(out=wu_raw[w][:, 2 * a : 2 * a + 2, :], in_=view[:, 2 * a : 2 * a + 2, :])
+            nc.sync.dma_start(out=wu_raw[w][:, :, 512 * c0 : 512 * c1], in_=view[:, :, 512 * c0 : 512 * c1])
+
+        def load_up(w):
+            nc.sync.dma_start(out=wu_raw[w][:], in_=(Wk_up, Wv_up)[w].rearrange("(p j) n -> p j n", j=4))
 
         load_wr()
         load_wkv(0)
@@ -110,15 +113,22 @@ def tile_multiheadlatentattention_pb_kernel(tc, inputs_k, Wkv_down, Wk_up, Wv_up
         load_x(1)
         load_x(2)
         load_x(3)
-        load_up(0, 0)
-        load_up(0, 1)
-        load_up(1, 0)
-        load_up(1, 1)
+        load_up(0)
+        load_up(1)
 
         pos_i = const.tile([P, 2], I32)
         nc.gpsimd.iota(pos_i[:], pattern=[[P, 2]], base=0, channel_multiplier=1)
         ident = const.tile([P, P], F32)
         make_identity(nc, ident[:])
+
+        zero_w = const.tile([P, P], BF16)
+        nc.vector.memset(zero_w[:], 0.0)
+
+        r_bank = [psr.tile([P, 512], F32, name="r_bank%d" % b) for b in range(2)]
+
+        def keep_warm(src):
+            for rep in range(2):
+                nc.tensor.matmul(out=r_bank[1][:], lhsT=zero_w[:], rhs=src, start=True, stop=True)
 
         warm = const.tile([P, 1], F32)
         nc.vector.memset(warm[:], 0.0)
@@ -229,23 +239,29 @@ def tile_multiheadlatentattention_pb_kernel(tc, inputs_k, Wkv_down, Wk_up, Wv_up
         xs = [keep.tile([P, G * P], U8, name="xs%d" % m, align_bytes=64) for m in range(TT)]
         lc = [keep.tile([P, P], U32, name="lc%d" % m, align_bytes=64) for m in range(TT)]
         ls = [keep.tile([P, P], U8, name="ls%d" % m, align_bytes=64) for m in range(TT)]
-        r_ps = [psr.tile([P, 2 * HD], F32, name="r_ps%d" % b) for b in range(2)]
+        r_ps = [r_bank[b][:, 0 : 2 * HD] for b in range(2)]
         rope = [const.tile([P, 2 * HD], F32, name="rope%d" % b) for b in range(2)]
         x_grp = {}
         l_grp = {}
 
-        def x_in(m, copies):
+        x_ps = {}
+
+        def x_turn(m):
             xw = xr[m // 2][:, m % 2, :].bitcast(F32)
-            gx = grp.tile([P, 2048], BF16, tag="grp", name="gx%d" % m, align_bytes=64)
-            x_grp[m] = gx
-            gxw = gx[:].bitcast(F32).rearrange("p (g r u) -> p g r u", g=G, u=2)
             for gp in range(2):
                 xt = ps.tile([P, 4, P], F32, tag="acc", name="xt")
+                x_ps[(m, gp)] = xt
                 for gi in range(2):
                     g = 2 * gp + gi
                     for u in range(2):
                         nc.tensor.transpose(xt[:, 2 * gi + u, :], xw[:, 256 * g + u : 256 * (g + 1) : 2], ident[:])
-                copies[gp](gxw[:, 2 * gp : 2 * gp + 2, :, :], xt[:].rearrange("p (g u) r -> p g r u", u=2))
+
+        def x_copy(m, copy):
+            gx = grp.tile([P, 2048], BF16, tag="grp", name="gx%d" % m, align_bytes=64)
+            x_grp[m] = gx
+            gxw = gx[:].bitcast(F32).rearrange("p (g r u) -> p g r u", g=G, u=2)
+            for gp in range(2):
+                copy(gxw[:, 2 * gp : 2 * gp + 2, :, :], x_ps[(m, gp)][:].rearrange("p (g u) r -> p g r u", u=2))
 
         def x_quant(m):
             quantise(xc[m][:], xs[m][:], x_grp[m][:])
@@ -273,9 +289,9 @@ def tile_multiheadlatentattention_pb_kernel(tc, inputs_k, Wkv_down, Wk_up, Wv_up
         def rotate(b):
             t1 = const.tile([P, 2 * HD], F32, name="t1_%d" % b)
             t2 = const.tile([P, 2, 2, 64], F32, name="t2_%d" % b)
-            rv = r_ps[b][:].rearrange("p (h f j) -> p h f j", h=2, f=2)
+            rv = r_ps[b].rearrange("p (h f j) -> p h f j", h=2, f=2)
             nc.vector.tensor_tensor(
-                out=t1[:], in0=r_ps[b][:], in1=cos2[:].rearrange("p h f j -> p (h f j)"), op=ALU.mult
+                out=t1[:], in0=r_ps[b], in1=cos2[:].rearrange("p h f j -> p (h f j)"), op=ALU.mult
             )
             for f in range(2):
                 nc.vector.tensor_tensor(out=t2[:, :, f, :], in0=rv[:, :, 1 - f, :], in1=sin2[:, :, f, :], op=ALU.mult)
@@ -300,18 +316,22 @@ def tile_multiheadlatentattention_pb_kernel(tc, inputs_k, Wkv_down, Wk_up, Wv_up
             quantise(wuc[c][:], wus[c][:], u_grp[c][:])
 
         vst = {}
-        kst = [[stage.tile([P, 4, 2 * HD], F32, name="kst%d_%d" % (m, par)) for par in range(2)] for m in range(TT)]
+        kst = [stage.tile([P, 8, 2 * HD], F32, name="kst%d" % m) for m in range(TT)]
 
-        def fill(m, par, copy):
+        def fill(m, h0, heads, copy):
             hs = slice(HD * (m % 2), HD * (m % 2 + 1))
-            copy(kst[m][par][:, :, HD : 2 * HD], rope[m // 2][:, hs].unsqueeze(1).to_broadcast([P, 4, HD]))
+            copy(
+                kst[m][:, h0 : h0 + heads, HD : 2 * HD],
+                rope[m // 2][:, hs].unsqueeze(1).to_broadcast([P, heads, HD]),
+            )
 
         def out_k(c, m, copy):
             rows = slice(P * m, P * (m + 1))
             o = ps.tile([P, 512], F32, tag="acc", name="o")
             mx(o[:], lc[m][:], ls[m][:], wuc[c][:], wus[c][:], True, True)
-            copy(kst[m][c % 2][:, :, 0:HD], o[:].rearrange("p (h d) -> p h d", h=4))
-            nc.sync.dma_start(out=k_out[rows, 4 * c : 4 * c + 4, :], in_=kst[m][c % 2][:])
+            h0 = 4 * (c % 2)
+            copy(kst[m][:, h0 : h0 + 4, 0:HD], o[:].rearrange("p (h d) -> p h d", h=4))
+            nc.sync.dma_start(out=k_out[rows, 4 * c : 4 * c + 4, :], in_=kst[m][:, h0 : h0 + 4, :])
 
         def out_v(c, m, copy):
             rows = slice(P * m, P * (m + 1))
@@ -332,49 +352,60 @@ def tile_multiheadlatentattention_pb_kernel(tc, inputs_k, Wkv_down, Wk_up, Wv_up
         wkv_quant(0)
         wkv_regroup(2, vcopy)
         trig()
-        wkv_regroup(3, scopy)
+        wkv_regroup(3, vcopy)
         wkv_quant(1)
         wkv_quant(2)
-        x_in(0, (scopy, vcopy))
+        x_turn(0)
+        x_copy(0, scopy)
         wkv_quant(3)
-        x_in(1, (scopy, vcopy))
+        x_turn(1)
+        x_copy(1, scopy)
         x_quant(0)
         finish_tables()
-        x_in(2, (scopy, vcopy))
+        x_turn(2)
+        x_copy(2, scopy)
         x_quant(1)
-        x_in(3, (scopy, vcopy))
+        x_turn(3)
+        x_copy(3, scopy)
+        rope_stage(0)
+        rope_stage(1)
         x_quant(2)
         first_stage(0, scopy)
-        rope_stage(0)
         x_quant(3)
+        rotate(0)
+        fill(0, 0, 4, scopy)
         first_stage(1, scopy)
-        rope_stage(1)
-        lat_quant(0)
+        fill(1, 0, 4, scopy)
         up_regroup(0, vcopy)
         first_stage(2, scopy)
         rope_stage(2)
-        lat_quant(1)
-        rotate(0)
-        up_quant(0)
-        first_stage(3, scopy)
         rope_stage(3)
+        lat_quant(0)
+        up_quant(0)
+        lat_quant(1)
+        out_k(0, 0, scopy)
+        out_k(0, 1, scopy)
+        rotate(1)
+        fill(2, 0, 4, scopy)
+        first_stage(3, scopy)
         lat_quant(2)
         up_regroup(1, vcopy)
+        out_k(0, 2, scopy)
+        fill(3, 0, 4, scopy)
         lat_quant(3)
-        fill(0, 0, scopy)
-        fill(1, 0, scopy)
-        rotate(1)
-        fill(2, 0, vcopy)
-        fill(3, 0, vcopy)
-        for c in range(8):
-            if 0 < c < 7:
+        up_quant(1)
+        out_k(0, 3, scopy)
+        fill(0, 4, 4, vcopy)
+        fill(1, 4, 4, vcopy)
+        fill(2, 4, 4, vcopy)
+        fill(3, 4, 4, vcopy)
+        for c in range(1, 8):
+            if c < 7:
                 up_regroup(c + 1, vcopy)
             for m in range(TT):
                 if c < 4:
                     out_k(c, m, scopy)
                 else:
                     out_v(c, m, scopy if m < 3 else vcopy)
-                if c == 0:
-                    fill(m, 1, scopy if m < 2 else vcopy)
             if c + 1 < 8:
                 up_quant(c + 1)

@@ -83,7 +83,7 @@ def tile_multiheadlatentattention_pb_kernel(tc, inputs_k, Wkv_down, Wk_up, Wv_up
         wr_raw = raw.tile([P, G, 4 * HD], BF16)
         wkr = [big.tile([P, 2, 4 * KL], BF16, tag="big", name="wkr%d" % i) for i in range(2)]
         xr = [big.tile([P, 2, D], BF16, tag="big", name="xr%d" % i) for i in range(2)]
-        wu_raw = [raw.tile([P, 4, D], BF16, name="wu_raw%d" % w) for w in range(2)]
+        wu_raw = [None, raw.tile([P, 4, D], BF16, name="wv_raw")]
 
         def load_wr():
             nc.sync.dma_start(out=wr_raw[:], in_=Wk_rope.rearrange("(g p j) c -> p g (j c)", g=G, j=4))
@@ -97,9 +97,14 @@ def tile_multiheadlatentattention_pb_kernel(tc, inputs_k, Wkv_down, Wk_up, Wv_up
         def load_x(m):
             nc.sync.dma_start(out=xr[m // 2][:, m % 2, :], in_=x[P * m : P * (m + 1), :])
 
-        def load_up_cols(w, c0, c1):
-            view = (Wk_up, Wv_up)[w].rearrange("(p j) n -> p j n", j=4)
-            nc.sync.dma_start(out=wu_raw[w][:, :, 512 * c0 : 512 * c1], in_=view[:, :, 512 * c0 : 512 * c1])
+        wk_first = raw.tile([P, 4, 512], BF16)
+        wk_rest = raw.tile([P, 4, D - 512], BF16)
+
+        def load_wk_first():
+            nc.sync.dma_start(out=wk_first[:], in_=Wk_up.rearrange("(p j) n -> p j n", j=4)[:, :, 0:512])
+
+        def load_wk_rest():
+            nc.sync.dma_start(out=wk_rest[:], in_=Wk_up.rearrange("(p j) n -> p j n", j=4)[:, :, 512:D])
 
         def load_up(w):
             nc.sync.dma_start(out=wu_raw[w][:], in_=(Wk_up, Wv_up)[w].rearrange("(p j) n -> p j n", j=4))
@@ -113,22 +118,14 @@ def tile_multiheadlatentattention_pb_kernel(tc, inputs_k, Wkv_down, Wk_up, Wv_up
         load_x(1)
         load_x(2)
         load_x(3)
-        load_up(0)
+        load_wk_first()
+        load_wk_rest()
         load_up(1)
 
         pos_i = const.tile([P, 2], I32)
         nc.gpsimd.iota(pos_i[:], pattern=[[P, 2]], base=0, channel_multiplier=1)
         ident = const.tile([P, P], F32)
         make_identity(nc, ident[:])
-
-        zero_w = const.tile([P, P], BF16)
-        nc.vector.memset(zero_w[:], 0.0)
-
-        r_bank = [psr.tile([P, 512], F32, name="r_bank%d" % b) for b in range(2)]
-
-        def keep_warm(src):
-            for rep in range(2):
-                nc.tensor.matmul(out=r_bank[1][:], lhsT=zero_w[:], rhs=src, start=True, stop=True)
 
         warm = const.tile([P, 1], F32)
         nc.vector.memset(warm[:], 0.0)
@@ -235,11 +232,22 @@ def tile_multiheadlatentattention_pb_kernel(tc, inputs_k, Wkv_down, Wk_up, Wv_up
                 out=sin2[:, :, 1, :], in0=sin_sq[:, 1, :, :], scalar1=-2.0, scalar2=1.0, op0=ALU.mult, op1=ALU.add
             )
 
+        def finish_tables_scalar():
+            nc.scalar.activation(
+                out=cos2[:],
+                in_=sin_sq[:, 0, :, :].unsqueeze(2).to_broadcast([P, 2, 2, 64]),
+                func=ACT.Copy,
+                scale=-2.0,
+                bias=1.0,
+            )
+            nc.scalar.activation(out=sin2[:, :, 0, :], in_=sin_sq[:, 1, :, :], func=ACT.Copy, scale=2.0, bias=-1.0)
+            nc.scalar.activation(out=sin2[:, :, 1, :], in_=sin_sq[:, 1, :, :], func=ACT.Copy, scale=-2.0, bias=1.0)
+
         xc = [keep.tile([P, G * P], U32, name="xc%d" % m, align_bytes=64) for m in range(TT)]
         xs = [keep.tile([P, G * P], U8, name="xs%d" % m, align_bytes=64) for m in range(TT)]
         lc = [keep.tile([P, P], U32, name="lc%d" % m, align_bytes=64) for m in range(TT)]
         ls = [keep.tile([P, P], U8, name="ls%d" % m, align_bytes=64) for m in range(TT)]
-        r_ps = [r_bank[b][:, 0 : 2 * HD] for b in range(2)]
+        r_ps = [psr.tile([P, 2 * HD], F32, name="r_ps%d" % b)[:] for b in range(2)]
         rope = [const.tile([P, 2 * HD], F32, name="rope%d" % b) for b in range(2)]
         x_grp = {}
         l_grp = {}
@@ -306,11 +314,13 @@ def tile_multiheadlatentattention_pb_kernel(tc, inputs_k, Wkv_down, Wk_up, Wv_up
         def up_regroup(c, copy):
             gu = grp.tile([P, 2048], BF16, tag="grp", name="gu%d" % c, align_bytes=64)
             u_grp[c] = gu
-            cc = c % 4
-            copy(
-                gu[:].rearrange("p (c i j) -> p c j i", i=4, j=4),
-                wu_raw[c // 4][:, :, 512 * cc : 512 * (cc + 1)].rearrange("p j (c i) -> p c j i", i=4),
-            )
+            if c == 0:
+                src = wk_first[:]
+            elif c < 4:
+                src = wk_rest[:, :, 512 * (c - 1) : 512 * c]
+            else:
+                src = wu_raw[1][:, :, 512 * (c - 4) : 512 * (c - 3)]
+            copy(gu[:].rearrange("p (c i j) -> p c j i", i=4, j=4), src.rearrange("p j (c i) -> p c j i", i=4))
 
         def up_quant(c):
             quantise(wuc[c][:], wus[c][:], u_grp[c][:])
@@ -352,6 +362,7 @@ def tile_multiheadlatentattention_pb_kernel(tc, inputs_k, Wkv_down, Wk_up, Wv_up
         wkv_quant(0)
         wkv_regroup(2, vcopy)
         trig()
+        finish_tables_scalar()
         wkv_regroup(3, vcopy)
         wkv_quant(1)
         wkv_quant(2)
@@ -361,7 +372,6 @@ def tile_multiheadlatentattention_pb_kernel(tc, inputs_k, Wkv_down, Wk_up, Wv_up
         x_turn(1)
         x_copy(1, scopy)
         x_quant(0)
-        finish_tables()
         x_turn(2)
         x_copy(2, scopy)
         x_quant(1)
@@ -369,32 +379,34 @@ def tile_multiheadlatentattention_pb_kernel(tc, inputs_k, Wkv_down, Wk_up, Wv_up
         x_copy(3, scopy)
         rope_stage(0)
         rope_stage(1)
+
+        up_regroup(0, vcopy)
         x_quant(2)
         first_stage(0, scopy)
-        x_quant(3)
         rotate(0)
         fill(0, 0, 4, scopy)
+        up_quant(0)
         first_stage(1, scopy)
         fill(1, 0, 4, scopy)
-        up_regroup(0, vcopy)
-        first_stage(2, scopy)
-        rope_stage(2)
-        rope_stage(3)
         lat_quant(0)
-        up_quant(0)
+        x_quant(3)
         lat_quant(1)
+        first_stage(2, scopy)
         out_k(0, 0, scopy)
         out_k(0, 1, scopy)
-        rotate(1)
-        fill(2, 0, 4, scopy)
+        rope_stage(2)
+        rope_stage(3)
         first_stage(3, scopy)
-        lat_quant(2)
         up_regroup(1, vcopy)
+        lat_quant(2)
+        rotate(1)
+        fill(2, 0, 4, vcopy)
         out_k(0, 2, scopy)
-        fill(3, 0, 4, scopy)
+        fill(3, 0, 4, vcopy)
         lat_quant(3)
         up_quant(1)
         out_k(0, 3, scopy)
+
         fill(0, 4, 4, vcopy)
         fill(1, 4, 4, vcopy)
         fill(2, 4, 4, vcopy)

@@ -301,8 +301,7 @@ def tile_multiheadlatentattention_pb_kernel(tc, inputs_k, Wkv_down, Wk_up, Wv_up
             nc.vector.tensor_tensor(
                 out=t1[:], in0=r_ps[b], in1=cos2[:].rearrange("p h f j -> p (h f j)"), op=ALU.mult
             )
-            for f in range(2):
-                nc.vector.tensor_tensor(out=t2[:, :, f, :], in0=rv[:, :, 1 - f, :], in1=sin2[:, :, f, :], op=ALU.mult)
+            nc.vector.tensor_tensor(out=t2[:], in0=rv[:, :, ::-1, :], in1=sin2[:], op=ALU.mult)
             nc.vector.tensor_tensor(
                 out=rope[b][:], in0=t1[:], in1=t2[:].rearrange("p h f j -> p (h f j)"), op=ALU.add
             )

@@ -325,6 +325,9 @@ def tile_multiheadlatentattention_pb_kernel(tc, inputs_k, Wkv_down, Wk_up, Wv_up
             quantise(wuc[c][:], wus[c][:], u_grp[c][:])
 
         vst = {}
+        def token_rows(m):
+            return slice(P * m, P * (m + 1))
+
         kst = [stage.tile([P, 8, 2 * HD], F32, name="kst%d" % m) for m in range(TT)]
 
         def fill(m, h0, heads, copy):
@@ -340,7 +343,10 @@ def tile_multiheadlatentattention_pb_kernel(tc, inputs_k, Wkv_down, Wk_up, Wv_up
             mx(o[:], lc[m][:], ls[m][:], wuc[c][:], wus[c][:], True, True)
             h0 = 4 * (c % 2)
             copy(kst[m][:, h0 : h0 + 4, 0:HD], o[:].rearrange("p (h d) -> p h d", h=4))
-            nc.sync.dma_start(out=k_out[rows, 4 * c : 4 * c + 4, :], in_=kst[m][:, h0 : h0 + 4, :])
+            if c < 2:
+                nc.sync.dma_start(out=k_out[rows, 4 * c : 4 * c + 4, :], in_=kst[m][:, h0 : h0 + 4, :])
+            elif c == 3:
+                nc.sync.dma_start(out=k_out[rows, 8:16, :], in_=kst[m][:])
 
         def out_v(c, m, copy):
             rows = slice(P * m, P * (m + 1))
@@ -350,9 +356,9 @@ def tile_multiheadlatentattention_pb_kernel(tc, inputs_k, Wkv_down, Wk_up, Wv_up
                 vst[m] = big.tile([P, D], F32, tag="big", name="vst%d" % m)
             cc = c - 4
             copy(vst[m][:, 512 * cc : 512 * (cc + 1)], o[:])
-            if c % 2 == 1:
-                half = slice(1024 * (cc // 2), 1024 * (cc // 2 + 1))
-                nc.sync.dma_start(out=v_out[rows, half], in_=vst[m][:, half])
+
+        def store_v(m):
+            nc.sync.dma_start(out=v_out[token_rows(m), :], in_=vst[m][:])
 
         wr_regroup(scopy)
         wkv_regroup(0, vcopy)
@@ -406,17 +412,34 @@ def tile_multiheadlatentattention_pb_kernel(tc, inputs_k, Wkv_down, Wk_up, Wv_up
         up_quant(1)
         out_k(0, 3, scopy)
 
-        fill(0, 4, 4, vcopy)
-        fill(1, 4, 4, vcopy)
+        fill(0, 4, 4, scopy)
+        up_regroup(2, vcopy)
+        out_k(1, 0, scopy)
+        fill(1, 4, 4, scopy)
+        out_k(1, 1, scopy)
         fill(2, 4, 4, vcopy)
         fill(3, 4, 4, vcopy)
-        for c in range(1, 8):
-            if c < 7:
-                up_regroup(c + 1, vcopy)
-            for m in range(TT):
-                if c < 4:
-                    out_k(c, m, scopy)
-                else:
-                    out_v(c, m, scopy if m < 3 else vcopy)
-            if c + 1 < 8:
-                up_quant(c + 1)
+        out_k(1, 2, scopy)
+        out_k(1, 3, scopy)
+        up_regroup(3, vcopy)
+        up_quant(2)
+        up_quant(3)
+        up_regroup(4, vcopy)
+        for m in range(TT):
+            out_k(2, m, scopy)
+            out_k(3, m, scopy)
+        up_regroup(5, vcopy)
+        up_quant(4)
+        for m in range(TT):
+            out_v(4, m, scopy)
+        up_regroup(6, vcopy)
+        up_quant(5)
+        up_regroup(7, vcopy)
+        up_quant(6)
+        up_quant(7)
+        for m in range(2):
+            for c in range(5, 8):
+                out_v(c, m, scopy)
+                out_v(c, m + 2, vcopy)
+            store_v(m)
+            store_v(m + 2)

@@ -26,23 +26,6 @@ PI = 3.141592653589793
 FLOPS = 2 * TOKENS * (D * KL + 2 * KL * D + D * HD)
 
 
-def round_bits(x, bits):
-    if x == 0.0:
-        return 0.0
-    s = 1.0
-    a = abs(x)
-    while a * s < 2.0 ** (bits - 1):
-        s *= 2.0
-    while a * s >= 2.0 ** bits:
-        s *= 0.5
-    return round(x * s) / s
-
-
-QUARTER_PI_1 = round_bits(PI / 4.0, 16)
-QUARTER_PI_2 = round_bits(PI / 4.0 - QUARTER_PI_1, 16)
-QUARTER_PI_3 = round_bits(PI / 4.0 - QUARTER_PI_1 - QUARTER_PI_2, 24)
-
-
 def tile_multiheadlatentattention_pb_kernel(tc, inputs_k, Wkv_down, Wk_up, Wv_up, Wk_rope, out_0, out_1):
     nc = tc.nc
     x = inputs_k.flatten_outer_dims()
@@ -122,8 +105,10 @@ def tile_multiheadlatentattention_pb_kernel(tc, inputs_k, Wkv_down, Wk_up, Wv_up
         load_wk_rest()
         load_up(1)
 
-        pos_i = const.tile([P, 2], I32)
-        nc.gpsimd.iota(pos_i[:], pattern=[[P, 2]], base=0, channel_multiplier=1)
+        pos = const.tile([P, 2], F32)
+        nc.gpsimd.iota(
+            pos[:], pattern=[[P, 2]], base=0, channel_multiplier=1, allow_small_or_imprecise_dtypes=True
+        )
         ident = const.tile([P, P], F32)
         make_identity(nc, ident[:])
 
@@ -143,44 +128,28 @@ def tile_multiheadlatentattention_pb_kernel(tc, inputs_k, Wkv_down, Wk_up, Wv_up
                 scalar2=None,
                 op0=ALU.mult,
             )
-        pos = const.tile([P, 2], F32)
-        nc.vector.tensor_copy(out=pos[:], in_=pos_i[:])
         half_ang = const.tile([P, 2, 64], F32)
+        turns = const.tile([P, 2, 64], I32)
+        for h in range(2):
+            nc.vector.tensor_scalar(
+                out=turns[:, h, :],
+                in0=half_freq[:],
+                scalar1=pos[:, h : h + 1],
+                scalar2=1.0 / PI,
+                op0=ALU.mult,
+                op1=ALU.mult,
+            )
         for h in range(2):
             nc.vector.tensor_scalar(
                 out=half_ang[:, h, :], in0=half_freq[:], scalar1=pos[:, h : h + 1], scalar2=None, op0=ALU.mult
             )
-        ha = half_ang[:].rearrange("p h j -> p (h j)")
-        turns = const.tile([P, 2, P], F32)
-        nc.vector.tensor_scalar(out=turns[:, 0, :], in0=ha, scalar1=1.0 / PI, scalar2=None, op0=ALU.mult)
-        nc.vector.tensor_scalar(out=turns[:, 1, :], in0=ha, scalar1=1.0 / PI, scalar2=-0.25, op0=ALU.mult, op1=ALU.add)
-        turns_i = const.tile([P, 2, P], I32)
-        nc.vector.tensor_copy(out=turns_i[:], in_=turns[:])
-        quarters = const.tile([P, 2, P], F32)
-        nc.vector.tensor_scalar(out=quarters[:, 0, :], in0=turns_i[:, 0, :], scalar1=4.0, scalar2=None, op0=ALU.mult)
-        nc.vector.tensor_scalar(
-            out=quarters[:, 1, :], in0=turns_i[:, 1, :], scalar1=4.0, scalar2=1.0, op0=ALU.mult, op1=ALU.add
-        )
-        red1 = const.tile([P, 2, P], F32)
+        red = const.tile([P, 2, 64], F32)
         nc.vector.scalar_tensor_tensor(
-            out=red1[:],
-            in0=quarters[:],
-            scalar=-QUARTER_PI_1,
-            in1=ha.unsqueeze(1).to_broadcast([P, 2, P]),
-            op0=ALU.mult,
-            op1=ALU.add,
-        )
-        red2 = const.tile([P, 2, P], F32)
-        nc.vector.scalar_tensor_tensor(
-            out=red2[:], in0=quarters[:], scalar=-QUARTER_PI_2, in1=red1[:], op0=ALU.mult, op1=ALU.add
-        )
-        red3 = const.tile([P, 2, P], F32)
-        nc.vector.scalar_tensor_tensor(
-            out=red3[:], in0=quarters[:], scalar=-QUARTER_PI_3, in1=red2[:], op0=ALU.mult, op1=ALU.add
+            out=red[:], in0=turns[:], scalar=-PI, in1=half_ang[:], op0=ALU.mult, op1=ALU.add
         )
 
-        sin_half = const.tile([P, 2, P], F32)
-        sin_sq = const.tile([P, 2, 2, 64], F32)
+        sin_half = const.tile([P, 2, 64], F32)
+        sin_sq = const.tile([P, 2, 64], F32)
         cos2 = const.tile([P, 2, 2, 64], F32)
         sin2 = const.tile([P, 2, 2, 64], F32)
 
@@ -213,35 +182,17 @@ def tile_multiheadlatentattention_pb_kernel(tc, inputs_k, Wkv_down, Wk_up, Wv_up
             quantise(wkc[g][:], wks[g][:], w_grp[g][:])
 
         def trig():
-            nc.scalar.activation(out=sin_half[:], in_=red3[:], func=ACT.Sin)
-            nc.scalar.activation(out=sin_sq[:].rearrange("p c h j -> p c (h j)"), in_=sin_half[:], func=ACT.Square)
-
-        def finish_tables():
-            nc.vector.tensor_scalar(
-                out=cos2[:],
-                in0=sin_sq[:, 0, :, :].unsqueeze(2).to_broadcast([P, 2, 2, 64]),
-                scalar1=-2.0,
-                scalar2=1.0,
-                op0=ALU.mult,
-                op1=ALU.add,
-            )
-            nc.vector.tensor_scalar(
-                out=sin2[:, :, 0, :], in0=sin_sq[:, 1, :, :], scalar1=2.0, scalar2=-1.0, op0=ALU.mult, op1=ALU.add
-            )
-            nc.vector.tensor_scalar(
-                out=sin2[:, :, 1, :], in0=sin_sq[:, 1, :, :], scalar1=-2.0, scalar2=1.0, op0=ALU.mult, op1=ALU.add
-            )
-
-        def finish_tables_scalar():
+            nc.scalar.activation(out=sin_half[:], in_=red[:], func=ACT.Sin)
+            nc.scalar.activation(out=sin2[:, :, 0, :], in_=red[:], func=ACT.Sin, scale=-2.0)
+            nc.scalar.activation(out=sin2[:, :, 1, :], in_=red[:], func=ACT.Sin, scale=2.0)
+            nc.scalar.activation(out=sin_sq[:], in_=sin_half[:], func=ACT.Square)
             nc.scalar.activation(
                 out=cos2[:],
-                in_=sin_sq[:, 0, :, :].unsqueeze(2).to_broadcast([P, 2, 2, 64]),
+                in_=sin_sq[:].unsqueeze(2).to_broadcast([P, 2, 2, 64]),
                 func=ACT.Copy,
                 scale=-2.0,
                 bias=1.0,
             )
-            nc.scalar.activation(out=sin2[:, :, 0, :], in_=sin_sq[:, 1, :, :], func=ACT.Copy, scale=2.0, bias=-1.0)
-            nc.scalar.activation(out=sin2[:, :, 1, :], in_=sin_sq[:, 1, :, :], func=ACT.Copy, scale=-2.0, bias=1.0)
 
         xc = [keep.tile([P, G * P], U32, name="xc%d" % m, align_bytes=64) for m in range(TT)]
         xs = [keep.tile([P, G * P], U8, name="xs%d" % m, align_bytes=64) for m in range(TT)]
@@ -367,7 +318,6 @@ def tile_multiheadlatentattention_pb_kernel(tc, inputs_k, Wkv_down, Wk_up, Wv_up
         wkv_quant(0)
         wkv_regroup(2, vcopy)
         trig()
-        finish_tables_scalar()
         wkv_regroup(3, vcopy)
         wkv_quant(1)
         wkv_quant(2)

@@ -105,10 +105,8 @@ def tile_multiheadlatentattention_pb_kernel(tc, inputs_k, Wkv_down, Wk_up, Wv_up
         load_wk_rest()
         load_up(1)
 
-        pos = const.tile([P, 2], F32)
-        nc.gpsimd.iota(
-            pos[:], pattern=[[P, 2]], base=0, channel_multiplier=1, allow_small_or_imprecise_dtypes=True
-        )
+        pos_i = const.tile([P, 2], I32)
+        nc.gpsimd.iota(pos_i[:], pattern=[[P, 2]], base=0, channel_multiplier=1)
         ident = const.tile([P, P], F32)
         make_identity(nc, ident[:])
 
@@ -128,6 +126,8 @@ def tile_multiheadlatentattention_pb_kernel(tc, inputs_k, Wkv_down, Wk_up, Wv_up
                 scalar2=None,
                 op0=ALU.mult,
             )
+        pos = const.tile([P, 2], F32)
+        nc.vector.tensor_copy(out=pos[:], in_=pos_i[:])
         half_ang = const.tile([P, 2, 64], F32)
         turns = const.tile([P, 2, 64], I32)
         for h in range(2):
@@ -215,23 +215,30 @@ def tile_multiheadlatentattention_pb_kernel(tc, inputs_k, Wkv_down, Wk_up, Wv_up
                     for u in range(2):
                         nc.tensor.transpose(xt[:, 2 * gi + u, :], xw[:, 256 * g + u : 256 * (g + 1) : 2], ident[:])
 
-        def x_copy(m, copy):
+        def x_copy(m, *copies):
             gx = grp.tile([P, 2048], BF16, tag="grp", name="gx%d" % m, align_bytes=64)
             x_grp[m] = gx
             gxw = gx[:].bitcast(F32).rearrange("p (g r u) -> p g r u", g=G, u=2)
-            for gp in range(2):
+            for gp, copy in enumerate(copies):
                 copy(gxw[:, 2 * gp : 2 * gp + 2, :, :], x_ps[(m, gp)][:].rearrange("p (g u) r -> p g r u", u=2))
 
         def x_quant(m):
             quantise(xc[m][:], xs[m][:], x_grp[m][:])
 
-        def first_stage(m, copy):
-            lat = ps.tile([P, 4, P], F32, tag="acc", name="lat")
-            for t in range(4):
+        lats = {}
+
+        def first_stage(m, first=0, end=4):
+            if first == 0:
+                lats[m] = ps.tile([P, 4, P], F32, tag="acc", name="lat")
+            lat = lats[m]
+            for t in range(first, end):
                 ts = slice(P * t, P * (t + 1))
                 for g in range(G):
                     gs = slice(P * g, P * (g + 1))
                     mx(lat[:, t, :], wkc[g][:, ts], wks[g][:, ts], xc[m][:, gs], xs[m][:, gs], g == 0, g == G - 1)
+
+        def lat_copy(m, copy):
+            lat = lats[m]
             gl = stage.tile([P, 4 * P], BF16, name="gl%d" % m, align_bytes=64)
             l_grp[m] = gl
             copy(gl[:].rearrange("p (r t) -> p r t", t=4), lat[:].rearrange("p t r -> p r t"))
@@ -245,7 +252,9 @@ def tile_multiheadlatentattention_pb_kernel(tc, inputs_k, Wkv_down, Wk_up, Wv_up
         def lat_quant(m):
             quantise(lc[m][:], ls[m][:], l_grp[m][:])
 
-        def rotate(b):
+        rot = {}
+
+        def rotate_products(b):
             t1 = const.tile([P, 2 * HD], F32, name="t1_%d" % b)
             t2 = const.tile([P, 2, 2, 64], F32, name="t2_%d" % b)
             rv = r_ps[b].rearrange("p (h f j) -> p h f j", h=2, f=2)
@@ -253,6 +262,10 @@ def tile_multiheadlatentattention_pb_kernel(tc, inputs_k, Wkv_down, Wk_up, Wv_up
                 out=t1[:], in0=r_ps[b], in1=cos2[:].rearrange("p h f j -> p (h f j)"), op=ALU.mult
             )
             nc.vector.tensor_tensor(out=t2[:], in0=rv[:, :, ::-1, :], in1=sin2[:], op=ALU.mult)
+            rot[b] = (t1, t2)
+
+        def rotate_sum(b):
+            t1, t2 = rot[b]
             nc.vector.tensor_tensor(
                 out=rope[b][:], in0=t1[:], in1=t2[:].rearrange("p h f j -> p (h f j)"), op=ALU.add
             )
@@ -288,16 +301,27 @@ def tile_multiheadlatentattention_pb_kernel(tc, inputs_k, Wkv_down, Wk_up, Wv_up
                 rope[m // 2][:, hs].unsqueeze(1).to_broadcast([P, heads, HD]),
             )
 
-        def out_k(c, m, copy):
-            rows = slice(P * m, P * (m + 1))
+        outs = {}
+
+        def product(c, m):
             o = ps.tile([P, 512], F32, tag="acc", name="o")
             mx(o[:], lc[m][:], ls[m][:], wuc[c][:], wus[c][:], True, True)
+            outs[(c, m)] = o
+
+        def out_k(c, m, copy):
+            product(c, m)
+            copy_k(c, m, copy)
+
+        def copy_k(c, m, copy):
+            o = outs[(c, m)]
             h0 = 4 * (c % 2)
             copy(kst[m][:, h0 : h0 + 4, 0:HD], o[:].rearrange("p (h d) -> p h d", h=4))
-            if c < 2:
-                nc.sync.dma_start(out=k_out[rows, 4 * c : 4 * c + 4, :], in_=kst[m][:, h0 : h0 + 4, :])
-            elif c == 3:
-                nc.sync.dma_start(out=k_out[rows, 8:16, :], in_=kst[m][:])
+
+        def store_k(c, n, m):
+            h0 = 4 * (c % 2)
+            nc.sync.dma_start(
+                out=k_out[token_rows(m), 4 * c : 4 * (c + n), :], in_=kst[m][:, h0 : h0 + 4 * n, :]
+            )
 
         def out_v(c, m, copy):
             rows = slice(P * m, P * (m + 1))
@@ -322,55 +346,68 @@ def tile_multiheadlatentattention_pb_kernel(tc, inputs_k, Wkv_down, Wk_up, Wv_up
         wkv_quant(1)
         wkv_quant(2)
         x_turn(0)
-        x_copy(0, scopy)
+        x_copy(0, scopy, scopy)
         wkv_quant(3)
         x_turn(1)
-        x_copy(1, scopy)
+        x_copy(1, scopy, scopy)
         x_quant(0)
         x_turn(2)
-        x_copy(2, scopy)
+        x_copy(2, scopy, scopy)
         x_quant(1)
         x_turn(3)
-        x_copy(3, scopy)
+        x_copy(3, scopy, scopy)
         rope_stage(0)
         rope_stage(1)
-
         up_regroup(0, vcopy)
+        rotate_products(0)
         x_quant(2)
-        first_stage(0, scopy)
-        rotate(0)
+        first_stage(0)
+        lat_copy(0, scopy)
+        rotate_sum(0)
         fill(0, 0, 4, scopy)
         up_quant(0)
-        first_stage(1, scopy)
+        first_stage(1)
+        lat_copy(1, scopy)
         fill(1, 0, 4, scopy)
         lat_quant(0)
         x_quant(3)
         lat_quant(1)
-        first_stage(2, scopy)
+        first_stage(2)
+        lat_copy(2, scopy)
         out_k(0, 0, scopy)
+        store_k(0, 1, 0)
         out_k(0, 1, scopy)
+        store_k(0, 1, 1)
         rope_stage(2)
         rope_stage(3)
-        first_stage(3, scopy)
+        first_stage(3)
+        lat_copy(3, scopy)
         up_regroup(1, vcopy)
+        rotate_products(1)
         lat_quant(2)
-        rotate(1)
+        rotate_sum(1)
+        product(0, 2)
         fill(2, 0, 4, vcopy)
-        out_k(0, 2, scopy)
+        copy_k(0, 2, scopy)
+        store_k(0, 1, 2)
         fill(3, 0, 4, vcopy)
         lat_quant(3)
         up_quant(1)
         out_k(0, 3, scopy)
-
+        store_k(0, 1, 3)
         fill(0, 4, 4, scopy)
         up_regroup(2, vcopy)
         out_k(1, 0, scopy)
+        store_k(1, 1, 0)
         fill(1, 4, 4, scopy)
         out_k(1, 1, scopy)
+        store_k(1, 1, 1)
         fill(2, 4, 4, vcopy)
         fill(3, 4, 4, vcopy)
         out_k(1, 2, scopy)
+        store_k(1, 1, 2)
         out_k(1, 3, scopy)
+        store_k(1, 1, 3)
         up_regroup(3, vcopy)
         up_quant(2)
         up_quant(3)
@@ -378,6 +415,7 @@ def tile_multiheadlatentattention_pb_kernel(tc, inputs_k, Wkv_down, Wk_up, Wv_up
         for m in range(TT):
             out_k(2, m, scopy)
             out_k(3, m, scopy)
+            store_k(2, 2, m)
         up_regroup(5, vcopy)
         up_quant(4)
         for m in range(TT):

from contextlib import ExitStack

import concourse.mybir as mybir
from concourse.masks import make_identity

F32 = mybir.dt.float32
BF16 = mybir.dt.bfloat16
I32 = mybir.dt.int32
U32 = mybir.dt.uint32
U8 = mybir.dt.uint8
FP8X4 = mybir.dt.float8_e4m3fn_x4
ALU = mybir.AluOpType
ACT = mybir.ActivationFunctionType

P = 128
TOKENS = 512
TT = 4
D = 2048
G = 4
KL = 512
HD = 128
HEADS = 16
ROPE_BASE = 10000.0
PI = 3.141592653589793

FLOPS = 2 * TOKENS * (D * KL + 2 * KL * D + D * HD)


def tile_multiheadlatentattention_pb_kernel(tc, inputs_k, Wkv_down, Wk_up, Wv_up, Wk_rope, out_0, out_1):
    nc = tc.nc
    x = inputs_k.flatten_outer_dims()
    k_out = out_0.rearrange("b s h d -> (b s) h d")
    v_out = out_1.rearrange("b s h d -> (b s) (h d)")

    with ExitStack() as ctx:
        ctx.enter_context(tc.manual_schedule())
        const = ctx.enter_context(tc.tile_pool(name="const", bufs=1))
        raw = ctx.enter_context(tc.tile_pool(name="raw", bufs=1))
        big = ctx.enter_context(tc.tile_pool(name="big", bufs=4))
        grp = ctx.enter_context(tc.tile_pool(name="grp", bufs=4))
        keep = ctx.enter_context(tc.tile_pool(name="keep", bufs=1))
        stage = ctx.enter_context(tc.tile_pool(name="stage", bufs=1))
        ps = ctx.enter_context(tc.psum_pool(name="ps", bufs=6))
        psr = ctx.enter_context(tc.psum_pool(name="psr", bufs=1))

        def vcopy(out, in_):
            nc.vector.tensor_copy(out=out, in_=in_)

        def scopy(out, in_):
            nc.scalar.copy(out=out, in_=in_)

        def quantise(codes, scales, in_):
            nc.vector.quantize_mx(out=codes.bitcast(FP8X4), scales=scales, in_=in_)

        def mx(out, a_codes, a_scales, b_codes, b_scales, start, stop):
            nc.tensor.matmul_mx(
                out=out,
                lhsT=a_codes.bitcast(FP8X4),
                lhsT_scale=a_scales,
                rhs=b_codes.bitcast(FP8X4),
                rhs_scale=b_scales,
                start=start,
                stop=stop,
            )

        wr_raw = raw.tile([P, G, 4 * HD], BF16)
        wkr = [big.tile([P, 2, 4 * KL], BF16, tag="big", name="wkr%d" % i) for i in range(2)]
        xr = [big.tile([P, 2, D], BF16, tag="big", name="xr%d" % i) for i in range(2)]
        wu_raw = [None, raw.tile([P, 4, D], BF16, name="wv_raw")]

        def load_wr():
            nc.sync.dma_start(out=wr_raw[:], in_=Wk_rope.rearrange("(g p j) c -> p g (j c)", g=G, j=4))

        def load_wkv(g):
            nc.sync.dma_start(
                out=wkr[g // 2][:, g % 2, :],
                in_=Wkv_down[512 * g : 512 * (g + 1), :].rearrange("(p j) c -> p (j c)", j=4),
            )

        def load_x(m):
            nc.sync.dma_start(out=xr[m // 2][:, m % 2, :], in_=x[P * m : P * (m + 1), :])

        wk_first = raw.tile([P, 4, 512], BF16)
        wk_rest = raw.tile([P, 4, D - 512], BF16)

        def load_wk_first():
            nc.sync.dma_start(out=wk_first[:], in_=Wk_up.rearrange("(p j) n -> p j n", j=4)[:, :, 0:512])

        def load_wk_rest():
            nc.sync.dma_start(out=wk_rest[:], in_=Wk_up.rearrange("(p j) n -> p j n", j=4)[:, :, 512:D])

        def load_up(w):
            nc.sync.dma_start(out=wu_raw[w][:], in_=(Wk_up, Wv_up)[w].rearrange("(p j) n -> p j n", j=4))

        load_wr()
        load_wkv(0)
        load_wkv(1)
        load_wkv(2)
        load_wkv(3)
        load_x(0)
        load_x(1)
        load_x(2)
        load_x(3)
        load_wk_first()
        load_wk_rest()
        load_up(1)

        pos_i = const.tile([P, 2], I32)
        nc.gpsimd.iota(pos_i[:], pattern=[[P, 2]], base=0, channel_multiplier=1)
        ident = const.tile([P, P], F32)
        make_identity(nc, ident[:])

        warm = const.tile([P, 1], F32)
        nc.vector.memset(warm[:], 0.0)
        warm_out = const.tile([P, 1], F32)
        nc.scalar.activation(out=warm_out[:], in_=warm[:], func=ACT.Sin)

        half_freq = const.tile([P, 64], F32)
        nc.vector.memset(half_freq[:, 0:1], 0.5)
        for e in range(6):
            w = 1 << e
            nc.vector.tensor_scalar(
                out=half_freq[:, w : 2 * w],
                in0=half_freq[:, 0:w],
                scalar1=ROPE_BASE ** (-w / 64.0),
                scalar2=None,
                op0=ALU.mult,
            )
        pos = const.tile([P, 2], F32)
        nc.vector.tensor_copy(out=pos[:], in_=pos_i[:])
        half_ang = const.tile([P, 2, 64], F32)
        turns = const.tile([P, 2, 64], I32)
        for h in range(2):
            nc.vector.tensor_scalar(
                out=turns[:, h, :],
                in0=half_freq[:],
                scalar1=pos[:, h : h + 1],
                scalar2=1.0 / PI,
                op0=ALU.mult,
                op1=ALU.mult,
            )
        for h in range(2):
            nc.vector.tensor_scalar(
                out=half_ang[:, h, :], in0=half_freq[:], scalar1=pos[:, h : h + 1], scalar2=None, op0=ALU.mult
            )
        red = const.tile([P, 2, 64], F32)
        nc.vector.scalar_tensor_tensor(
            out=red[:], in0=turns[:], scalar=-PI, in1=half_ang[:], op0=ALU.mult, op1=ALU.add
        )

        sin_half = const.tile([P, 2, 64], F32)
        sin_sq = const.tile([P, 2, 64], F32)
        cos2 = const.tile([P, 2, 2, 64], F32)
        sin2 = const.tile([P, 2, 2, 64], F32)

        wr_grp = keep.tile([P, 2048], BF16, align_bytes=64)
        wrc = keep.tile([P, G * HD], U32, align_bytes=64)
        wrs = keep.tile([P, G * HD], U8, align_bytes=64)

        def wr_regroup(copy):
            copy(
                wr_grp[:].rearrange("p (g c j) -> p g c j", g=G, j=4),
                wr_raw[:].rearrange("p g (j c) -> p g c j", j=4),
            )

        def wr_quant():
            quantise(wrc[:], wrs[:], wr_grp[:])

        wkc = [keep.tile([P, KL], U32, name="wkc%d" % g, align_bytes=64) for g in range(G)]
        wks = [keep.tile([P, KL], U8, name="wks%d" % g, align_bytes=64) for g in range(G)]
        w_grp = {}

        def wkv_regroup(g, copy):
            gw = grp.tile([P, 2048], BF16, tag="grp", name="gw%d" % g, align_bytes=64)
            w_grp[g] = gw
            copy(
                gw[:].rearrange("p (i q j) -> p q j i", i=4, j=4),
                wkr[g // 2][:, g % 2, :].rearrange("p (j q i) -> p q j i", j=4, i=4),
            )

        def wkv_quant(g):
            quantise(wkc[g][:], wks[g][:], w_grp[g][:])

        def trig():
            nc.scalar.activation(out=sin_half[:], in_=red[:], func=ACT.Sin)
            nc.scalar.activation(out=sin2[:, :, 0, :], in_=red[:], func=ACT.Sin, scale=-2.0)
            nc.scalar.activation(out=sin2[:, :, 1, :], in_=red[:], func=ACT.Sin, scale=2.0)
            nc.scalar.activation(out=sin_sq[:], in_=sin_half[:], func=ACT.Square)
            nc.scalar.activation(
                out=cos2[:],
                in_=sin_sq[:].unsqueeze(2).to_broadcast([P, 2, 2, 64]),
                func=ACT.Copy,
                scale=-2.0,
                bias=1.0,
            )

        xc = [keep.tile([P, G * P], U32, name="xc%d" % m, align_bytes=64) for m in range(TT)]
        xs = [keep.tile([P, G * P], U8, name="xs%d" % m, align_bytes=64) for m in range(TT)]
        lc = [keep.tile([P, P], U32, name="lc%d" % m, align_bytes=64) for m in range(TT)]
        ls = [keep.tile([P, P], U8, name="ls%d" % m, align_bytes=64) for m in range(TT)]
        r_ps = [psr.tile([P, 2 * HD], F32, name="r_ps%d" % b)[:] for b in range(2)]
        rope = [const.tile([P, 2 * HD], F32, name="rope%d" % b) for b in range(2)]
        x_grp = {}
        l_grp = {}

        x_ps = {}

        def x_turn(m):
            xw = xr[m // 2][:, m % 2, :].bitcast(F32)
            for gp in range(2):
                xt = ps.tile([P, 4, P], F32, tag="acc", name="xt")
                x_ps[(m, gp)] = xt
                for gi in range(2):
                    g = 2 * gp + gi
                    for u in range(2):
                        nc.tensor.transpose(xt[:, 2 * gi + u, :], xw[:, 256 * g + u : 256 * (g + 1) : 2], ident[:])

        def x_copy(m, *copies):
            gx = grp.tile([P, 2048], BF16, tag="grp", name="gx%d" % m, align_bytes=64)
            x_grp[m] = gx
            gxw = gx[:].bitcast(F32).rearrange("p (g r u) -> p g r u", g=G, u=2)
            for gp, copy in enumerate(copies):
                copy(gxw[:, 2 * gp : 2 * gp + 2, :, :], x_ps[(m, gp)][:].rearrange("p (g u) r -> p g r u", u=2))

        def x_quant(m):
            quantise(xc[m][:], xs[m][:], x_grp[m][:])

        lats = {}

        def first_stage(m, first=0, end=4):
            if first == 0:
                lats[m] = ps.tile([P, 4, P], F32, tag="acc", name="lat")
            lat = lats[m]
            for t in range(first, end):
                ts = slice(P * t, P * (t + 1))
                for g in range(G):
                    gs = slice(P * g, P * (g + 1))
                    mx(lat[:, t, :], wkc[g][:, ts], wks[g][:, ts], xc[m][:, gs], xs[m][:, gs], g == 0, g == G - 1)

        def lat_copy(m, copy):
            lat = lats[m]
            gl = stage.tile([P, 4 * P], BF16, name="gl%d" % m, align_bytes=64)
            l_grp[m] = gl
            copy(gl[:].rearrange("p (r t) -> p r t", t=4), lat[:].rearrange("p t r -> p r t"))

        def rope_stage(m):
            hs = slice(HD * (m % 2), HD * (m % 2 + 1))
            for g in range(G):
                gs = slice(P * g, P * (g + 1))
                mx(r_ps[m // 2][:, hs], xc[m][:, gs], xs[m][:, gs], wrc[:, gs], wrs[:, gs], g == 0, g == G - 1)

        def lat_quant(m):
            quantise(lc[m][:], ls[m][:], l_grp[m][:])

        rot = {}

        def rotate_products(b):
            t1 = const.tile([P, 2 * HD], F32, name="t1_%d" % b)
            t2 = const.tile([P, 2, 2, 64], F32, name="t2_%d" % b)
            rv = r_ps[b].rearrange("p (h f j) -> p h f j", h=2, f=2)
            nc.vector.tensor_tensor(
                out=t1[:], in0=r_ps[b], in1=cos2[:].rearrange("p h f j -> p (h f j)"), op=ALU.mult
            )
            nc.vector.tensor_tensor(out=t2[:], in0=rv[:, :, ::-1, :], in1=sin2[:], op=ALU.mult)
            rot[b] = (t1, t2)

        def rotate_sum(b):
            t1, t2 = rot[b]
            nc.vector.tensor_tensor(
                out=rope[b][:], in0=t1[:], in1=t2[:].rearrange("p h f j -> p (h f j)"), op=ALU.add
            )

        wuc = [keep.tile([P, 512], U32, name="wuc%d" % c, align_bytes=64) for c in range(8)]
        wus = [keep.tile([P, 512], U8, name="wus%d" % c, align_bytes=64) for c in range(8)]
        u_grp = {}

        def up_regroup(c, copy):
            gu = grp.tile([P, 2048], BF16, tag="grp", name="gu%d" % c, align_bytes=64)
            u_grp[c] = gu
            if c == 0:
                src = wk_first[:]
            elif c < 4:
                src = wk_rest[:, :, 512 * (c - 1) : 512 * c]
            else:
                src = wu_raw[1][:, :, 512 * (c - 4) : 512 * (c - 3)]
            copy(gu[:].rearrange("p (c i j) -> p c j i", i=4, j=4), src.rearrange("p j (c i) -> p c j i", i=4))

        def up_quant(c):
            quantise(wuc[c][:], wus[c][:], u_grp[c][:])

        vst = {}
        def token_rows(m):
            return slice(P * m, P * (m + 1))

        kst = [stage.tile([P, 8, 2 * HD], F32, name="kst%d" % m) for m in range(TT)]

        def fill(m, h0, heads, copy):
            hs = slice(HD * (m % 2), HD * (m % 2 + 1))
            copy(
                kst[m][:, h0 : h0 + heads, HD : 2 * HD],
                rope[m // 2][:, hs].unsqueeze(1).to_broadcast([P, heads, HD]),
            )

        outs = {}

        def product(c, m):
            o = ps.tile([P, 512], F32, tag="acc", name="o")
            mx(o[:], lc[m][:], ls[m][:], wuc[c][:], wus[c][:], True, True)
            outs[(c, m)] = o

        def out_k(c, m, copy):
            product(c, m)
            copy_k(c, m, copy)

        def copy_k(c, m, copy):
            o = outs[(c, m)]
            h0 = 4 * (c % 2)
            copy(kst[m][:, h0 : h0 + 4, 0:HD], o[:].rearrange("p (h d) -> p h d", h=4))

        def store_k(c, n, m):
            h0 = 4 * (c % 2)
            nc.sync.dma_start(
                out=k_out[token_rows(m), 4 * c : 4 * (c + n), :], in_=kst[m][:, h0 : h0 + 4 * n, :]
            )

        def out_v(c, m, copy):
            rows = slice(P * m, P * (m + 1))
            o = ps.tile([P, 512], F32, tag="acc", name="o")
            mx(o[:], lc[m][:], ls[m][:], wuc[c][:], wus[c][:], True, True)
            if c == 4:
                vst[m] = big.tile([P, D], F32, tag="big", name="vst%d" % m)
            cc = c - 4
            copy(vst[m][:, 512 * cc : 512 * (cc + 1)], o[:])

        def store_v(m):
            nc.sync.dma_start(out=v_out[token_rows(m), :], in_=vst[m][:])

        wr_regroup(scopy)
        wkv_regroup(0, vcopy)
        wkv_regroup(1, scopy)
        wr_quant()
        wkv_quant(0)
        wkv_regroup(2, vcopy)
        trig()
        wkv_regroup(3, vcopy)
        wkv_quant(1)
        wkv_quant(2)
        x_turn(0)
        x_copy(0, scopy, scopy)
        wkv_quant(3)
        x_turn(1)
        x_copy(1, scopy, scopy)
        x_quant(0)
        x_turn(2)
        x_copy(2, scopy, scopy)
        x_quant(1)
        x_turn(3)
        x_copy(3, scopy, scopy)
        rope_stage(0)
        rope_stage(1)
        up_regroup(0, vcopy)
        rotate_products(0)
        x_quant(2)
        first_stage(0)
        lat_copy(0, scopy)
        rotate_sum(0)
        fill(0, 0, 4, scopy)
        up_quant(0)
        first_stage(1)
        lat_copy(1, scopy)
        fill(1, 0, 4, scopy)
        lat_quant(0)
        x_quant(3)
        lat_quant(1)
        first_stage(2)
        lat_copy(2, scopy)
        out_k(0, 0, scopy)
        store_k(0, 1, 0)
        out_k(0, 1, scopy)
        store_k(0, 1, 1)
        rope_stage(2)
        rope_stage(3)
        first_stage(3)
        lat_copy(3, scopy)
        up_regroup(1, vcopy)
        rotate_products(1)
        lat_quant(2)
        rotate_sum(1)
        product(0, 2)
        fill(2, 0, 4, vcopy)
        copy_k(0, 2, scopy)
        store_k(0, 1, 2)
        fill(3, 0, 4, vcopy)
        lat_quant(3)
        up_quant(1)
        out_k(0, 3, scopy)
        store_k(0, 1, 3)
        fill(0, 4, 4, scopy)
        up_regroup(2, vcopy)
        out_k(1, 0, scopy)
        store_k(1, 1, 0)
        fill(1, 4, 4, scopy)
        out_k(1, 1, scopy)
        store_k(1, 1, 1)
        fill(2, 4, 4, vcopy)
        fill(3, 4, 4, vcopy)
        out_k(1, 2, scopy)
        store_k(1, 1, 2)
        out_k(1, 3, scopy)
        store_k(1, 1, 3)
        up_regroup(3, vcopy)
        up_quant(2)
        up_quant(3)
        up_regroup(4, vcopy)
        for m in range(TT):
            out_k(2, m, scopy)
            out_k(3, m, scopy)
            store_k(2, 2, m)
        up_regroup(5, vcopy)
        up_quant(4)
        for m in range(TT):
            out_v(4, m, scopy)
        up_regroup(6, vcopy)
        up_quant(5)
        up_regroup(7, vcopy)
        up_quant(6)
        up_quant(7)
        for m in range(2):
            for c in range(5, 8):
                out_v(c, m, scopy)
                out_v(c, m + 2, vcopy)
            store_v(m)
            store_v(m + 2)
